import numpy as np
import ml_dtypes


def mxq(x, axis, fmt="e4m3"):
    dtype, down = {"e4m3": (ml_dtypes.float8_e4m3fn, 7), "e5m2": (ml_dtypes.float8_e5m2, 14)}[fmt]
    v = np.moveaxis(np.asarray(x, np.float32).astype(ml_dtypes.bfloat16).astype(np.float64), axis, -1)
    blocks = v.reshape(v.shape[:-1] + (-1, 32))
    amax = np.abs(blocks).max(-1, keepdims=True)
    byte = np.maximum(np.where(amax > 0, np.frexp(amax)[1] - 1 + 127, 0) - down, 1)
    scale = np.exp2(byte - 127.0)
    codes = (blocks / scale).astype(np.float32).astype(dtype).astype(np.float64)
    return np.moveaxis((codes * scale).reshape(v.shape), -1, axis)


WIDE = False


def mx_kscale(k):
    if not WIDE:
        return np.ones(k)
    levels = np.array([10, -10, 5, -5, 0])
    a = np.random.permutation(np.resize(levels, k // 512 * 4)).reshape(k // 512, 4)
    idx = np.arange(k)
    return np.exp2(a[idx // 512, idx % 128 // 32])


BF16 = ml_dtypes.bfloat16


def bf(x):
    return np.asarray(x, np.float32).astype(BF16)


def f64(x):
    return np.asarray(x).astype(np.float64)


N, C, D, H, W = 4, 1, 1024, 32, 32
EPS = 1e-5


def setup_inputs():
    t = np.minimum(mx_kscale(D), 1.0) ** 2
    sig0 = 0.01 * (0.5 + np.random.random_sample((C, D)))
    sig = sig0 * t
    r = np.exp2(np.round(np.log2((sig / np.sqrt(sig**2 + EPS)) / (sig0 / np.sqrt(sig0**2 + EPS)))))
    mu = np.random.standard_normal((C, D))
    z = np.random.standard_normal((N, C, D, H, W))
    x = ((z + mu[None, :, :, None, None]) * sig[None, :, :, None, None]).reshape(N, C * D, H, W)
    weight = (np.eye(D)[None] + np.random.standard_normal((C, D, D)) / np.sqrt(D)) / r[:, None, :]
    return {"x": bf(x), "weight": bf(weight), "bias": bf(np.random.standard_normal(C * D) * 0.3)}


def reference(x, weight, bias):
    x, weight, bias = f64(x), f64(weight), f64(bias)
    n, cd, h, w = x.shape
    c = weight.shape[0]
    d = cd // c
    mean = np.mean(x, axis=(0, 2, 3), keepdims=True)
    var = np.mean(np.square(x - mean), axis=(0, 2, 3), keepdims=True)
    xn = (x - mean) / np.sqrt(var + EPS)
    xg = xn.reshape(n, c, d, h * w)
    out = mxq(weight, 2, "e4m3")[None] @ mxq(xg, 2, "e4m3")
    return out.reshape(n, cd, h, w) + bias[None, :, None, None]

@@ -1,0 +1,206 @@
+from contextlib import ExitStack
+
+import concourse.mybir as mybir
+from concourse.masks import make_identity
+
+F32 = mybir.dt.float32
+BF16 = mybir.dt.bfloat16
+U32 = mybir.dt.uint32
+U8 = mybir.dt.uint8
+FP8X4 = mybir.dt.float8_e4m3fn_x4
+ALU = mybir.AluOpType
+ACT = mybir.ActivationFunctionType
+AX = mybir.AxisListType
+
+P = 128
+NB = 4
+CH = 1024
+PX = 1024
+G = 2
+J = 4
+OB = CH // P
+PT = 512
+EPS = 1e-5
+COUNT = NB * PX
+FLOPS = 2 * CH * CH * NB * PX
+
+V_E = ()
+
+
+def tile_caps_bn_t_kernel(tc, x, weight, bias, out):
+    nc = tc.nc
+    x_v = x.rearrange("n (g p j) h w -> g n p j (h w)", g=G, p=P, j=J)
+    w_v = weight.rearrange("c (ob p) i -> p (c ob) i", p=P)
+    out_v = out.rearrange("n (ob p) h w -> n ob p (h w)", p=P)
+
+    with ExitStack() as ctx:
+        keep = ctx.enter_context(tc.tile_pool(name="keep", bufs=1))
+        xn_pool = ctx.enter_context(tc.tile_pool(name="xnp", bufs=3))
+        grp_pool = ctx.enter_context(tc.tile_pool(name="grpp", bufs=3))
+        q_pool = ctx.enter_context(tc.tile_pool(name="qp", bufs=6))
+        o_pool = ctx.enter_context(tc.tile_pool(name="op", bufs=8))
+        junk_pool = ctx.enter_context(tc.tile_pool(name="junkp", bufs=2))
+        psum = ctx.enter_context(tc.psum_pool(name="ps", bufs=8))
+
+        one = keep.tile([P, 1], F32, name="one")
+        nc.vector.memset(one[:], 1.0)
+        warm = keep.tile([P, 1], F32, name="warm")
+        nc.scalar.activation(out=warm[:], in_=one[:], func=ACT.Sqrt)
+        bz = keep.tile([P, P], BF16, name="bz")
+        nc.vector.memset(bz[:], 0.0)
+        ident_b = keep.tile([P, P], BF16, name="ident_b")
+        make_identity(nc, ident_b[:])
+        ident_f = keep.tile([P, P], F32, name="ident_f")
+        make_identity(nc, ident_f[:])
+
+        nc.scalar.dma_start(out=bz[0:OB, :], in_=bias.rearrange("(r c) -> r c", c=P))
+        xs = [[keep.tile([P, J, PX], BF16, name="x%d%d" % (g, n)) for n in range(NB)] for g in range(G)]
+        for g in range(G):
+            for n in range(NB):
+                if g == 0 and n == 0:
+                    nc.sync.dma_start(out=xs[g][n][:, 0:2, :], in_=x_v[g, n][:, 0:2, :])
+                    nc.sync.dma_start(out=xs[g][n][:, 2:4, :], in_=x_v[g, n][:, 2:4, :])
+                else:
+                    nc.sync.dma_start(out=xs[g][n][:], in_=x_v[g, n])
+        w_sb = [keep.tile([P, 2, CH], BF16, name="w%d" % a) for a in range(OB // 2)]
+        for a in range(OB // 2):
+            nc.sync.dma_start(out=w_sb[a][:], in_=w_v[:, 2 * a : 2 * a + 2, :])
+
+        bt = psum.tile([P, P], BF16, name="bt", tag="bank")
+        nc.tensor.transpose(bt[:], bz[:], ident_b[:])
+        bias_sb = keep.tile([P, OB], F32, name="bias_sb")
+        nc.vector.tensor_copy(out=bias_sb[:], in_=bt[:, 0:OB])
+
+        mv = keep.tile([P, G * J, 2], F32, name="mv")
+        rstd = keep.tile([P, G * J], F32, name="rstd")
+        for g in range(G):
+            st = keep.tile([P, 2, 2 * NB, 6], F32, name="st%d" % g)
+            negs = keep.tile([P, 2], F32, name="negs%d" % g)
+            acc = keep.tile([P, 2, NB], F32, name="acc%d" % g)
+            sx_ps = [psum.tile([P, PT], F32, name="sx%d%d" % (g, jj), tag="bank") for jj in range(2)]
+            nc.vector.tensor_scalar(
+                out=negs[:], in0=xs[g][0][:, 2:4, 0], scalar1=-1.0, scalar2=None, op0=ALU.mult
+            )
+            for n in range(NB):
+                for j in range(2):
+                    for h in range(2):
+                        nc.vector.bn_stats(
+                            out=st[:, j, 2 * n + h, :], in_=xs[g][n][:, j, PT * h : PT * h + PT]
+                        )
+                for jj in range(2):
+                    junk = junk_pool.tile([P, PX], BF16, name="junk", tag="junk")
+                    nc.scalar.activation(
+                        out=junk[:],
+                        in_=xs[g][n][:, 2 + jj, :],
+                        func=ACT.Square,
+                        bias=negs[:, jj : jj + 1],
+                        scale=1.0,
+                        accum_out=acc[:, jj, n : n + 1],
+                    )
+                    for h in range(2):
+                        nc.tensor.matmul(
+                            sx_ps[jj][:],
+                            lhsT=ident_b[:],
+                            rhs=xs[g][n][:, 2 + jj, PT * h : PT * h + PT],
+                            start=(n == 0 and h == 0),
+                            stop=(n == NB - 1 and h == 1),
+                        )
+            for j in range(2):
+                nc.vector.bn_aggr(out=mv[:, J * g + j, :], in_=st[:, j].rearrange("p a b -> p (a b)"))
+            sx = keep.tile([P, 2], F32, name="sxs%d" % g)
+            for jj in range(2):
+                nc.vector.tensor_reduce(out=sx[:, jj : jj + 1], in_=sx_ps[jj][:], op=ALU.add, axis=AX.X)
+            ssq = keep.tile([P, 2], F32, name="ssq%d" % g)
+            nc.vector.tensor_reduce(out=ssq[:], in_=acc[:], op=ALU.add, axis=AX.X)
+            mean_s = mv[:, J * g + 2 : J * g + 4, 0]
+            nc.vector.tensor_scalar(out=mean_s, in0=sx[:], scalar1=1.0 / COUNT, scalar2=None, op0=ALU.mult)
+            dd = keep.tile([P, 2], F32, name="dd%d" % g)
+            nc.vector.tensor_tensor(out=dd[:], in0=mean_s, in1=negs[:], op=ALU.add)
+            d2 = keep.tile([P, 2], F32, name="d2%d" % g)
+            nc.vector.tensor_tensor(out=d2[:], in0=dd[:], in1=dd[:], op=ALU.mult)
+            nc.vector.scalar_tensor_tensor(
+                out=mv[:, J * g + 2 : J * g + 4, 1],
+                in0=ssq[:],
+                scalar=1.0 / COUNT,
+                in1=d2[:],
+                op0=ALU.mult,
+                op1=ALU.subtract,
+            )
+            ve = keep.tile([P, J], F32, name="ve%d" % g)
+            nc.vector.tensor_scalar(
+                out=ve[:], in0=mv[:, J * g : J * g + J, 1], scalar1=EPS, scalar2=None, op0=ALU.add
+            )
+            sd = keep.tile([P, J], F32, name="sd%d" % g)
+            nc.scalar.activation(out=sd[:], in_=ve[:], func=ACT.Sqrt)
+            nc.vector.reciprocal(out=rstd[:, J * g : J * g + J], in_=sd[:])
+
+        wg = [keep.tile([P, CH * J], BF16, name="wg%d" % g, align_bytes=64) for g in range(G)]
+        wq = [keep.tile([P, CH], U32, name="wq%d" % g, align_bytes=64) for g in range(G)]
+        wsc = [keep.tile([P, CH], U8, name="wsc%d" % g, align_bytes=64) for g in range(G)]
+        for a in range(OB // 2):
+            words = w_sb[a][:].bitcast(F32).rearrange("p l (g v u) -> p l g u v", g=G, u=2)
+            for g in range(G):
+                wt = psum.tile([P, 2, 2, P], F32, name="wt", tag="bank")
+                for l in range(2):
+                    for u in range(2):
+                        nc.tensor.transpose(wt[:, l, u, :], words[:, l, g, u, :], ident_f[:])
+                dst = wg[g][:].bitcast(F32).rearrange("p (o u) -> p o u", u=2)[:, 256 * a : 256 * a + 256, :]
+                nc.scalar.copy(
+                    out=dst.rearrange("p (l o) u -> p l o u", l=2),
+                    in_=wt[:].rearrange("p l u o -> p l o u"),
+                )
+            for g in range(G):
+                nc.vector.quantize_mx(
+                    out=wq[g][:, 256 * a : 256 * a + 256].bitcast(FP8X4),
+                    scales=wsc[g][:, 256 * a : 256 * a + 256],
+                    in_=wg[g][:, 1024 * a : 1024 * a + 1024],
+                )
+
+        for pt in range(NB * PX // PT):
+            n, h = pt // 2, pt % 2
+            xq, xsc = [], []
+            for g in range(G):
+                xn = xn_pool.tile([P, J, PT], BF16, name="xn", tag="xn")
+                for j in range(J):
+                    nc.vector.tensor_scalar(
+                        out=xn[:, j, :],
+                        in0=xs[g][n][:, j, PT * h : PT * h + PT],
+                        scalar1=mv[:, J * g + j, 0:1],
+                        scalar2=rstd[:, J * g + j : J * g + j + 1],
+                        op0=ALU.subtract,
+                        op1=ALU.mult,
+                    )
+                grp = grp_pool.tile([P, PT, J], BF16, name="grp", tag="grp", align_bytes=64)
+                nc.vector.tensor_copy(
+                    out=grp[:].rearrange("p (c i) t -> p c t i", i=4),
+                    in_=xn[:].rearrange("p t (c i) -> p c t i", i=4),
+                )
+                q = q_pool.tile([P, PT], U32, name="xq", tag="xq", align_bytes=64)
+                s = q_pool.tile([P, PT], U8, name="xsc", tag="xsc", align_bytes=64)
+                nc.vector.quantize_mx(
+                    out=q[:].bitcast(FP8X4), scales=s[:], in_=grp[:].rearrange("p w t -> p (w t)")
+                )
+                xq.append(q)
+                xsc.append(s)
+            for ob in range(OB):
+                acc_ps = psum.tile([P, PT], F32, name="mm", tag="bank")
+                for g in range(G):
+                    nc.tensor.matmul_mx(
+                        out=acc_ps[:],
+                        lhsT=wq[g][:, P * ob : P * ob + P].bitcast(FP8X4),
+                        lhsT_scale=wsc[g][:, P * ob : P * ob + P],
+                        rhs=xq[g][:].bitcast(FP8X4),
+                        rhs_scale=xsc[g][:],
+                        start=(g == 0),
+                        stop=(g == G - 1),
+                    )
+                ot = o_pool.tile([P, PT], F32, name="ot", tag="ot")
+                if ob in V_E:
+                    nc.vector.tensor_scalar(
+                        out=ot[:], in0=acc_ps[:], scalar1=bias_sb[:, ob : ob + 1], scalar2=None, op0=ALU.add
+                    )
+                else:
+                    nc.scalar.activation(
+                        out=ot[:], in_=acc_ps[:], func=ACT.Identity, bias=bias_sb[:, ob : ob + 1], scale=1.0
+                    )
+                nc.sync.dma_start(out=out_v[n, ob][:, PT * h : PT * h + PT], in_=ot[:])

@@ -20,187 +20,293 @@ G = 2
 J = 4
 OB = CH // P
 PT = 512
+NU = NB * PX // PT
 EPS = 1e-5
 COUNT = NB * PX
 FLOPS = 2 * CH * CH * NB * PX
 
-V_E = ()
+XT_PITCH = 136
+N_XT = 4
+PIECES = (
+    ((0, 0, 512), (0, 512, 512), (1, 0, 1024), (2, 0, 1024), (3, 0, 1024)),
+    ((0, 0, 1024), (1, 0, 1024), (2, 0, 1024), (3, 0, 512), (3, 512, 512)),
+)
+BN_J = ((0, 1), (0,))
+T_BANKS = (5, 6, 7)
+WT_BANKS = (5, 6, 7, 0, 1, 5, 6, 7)
 
 
 def tile_caps_bn_t_kernel(tc, x, weight, bias, out):
     nc = tc.nc
     x_v = x.rearrange("n (g p j) h w -> g n p j (h w)", g=G, p=P, j=J)
-    w_v = weight.rearrange("c (ob p) i -> p (c ob) i", p=P)
-    out_v = out.rearrange("n (ob p) h w -> n ob p (h w)", p=P)
+    w_v = weight.rearrange("c (p ob) i -> p (c ob) i", ob=OB)
+    b_v = bias.rearrange("(p ob) -> p ob", ob=OB)
+    out_v = out.rearrange("n (p ob) h w -> n p ob (h w)", ob=OB)
 
     with ExitStack() as ctx:
+        ctx.enter_context(tc.manual_schedule())
         keep = ctx.enter_context(tc.tile_pool(name="keep", bufs=1))
-        xn_pool = ctx.enter_context(tc.tile_pool(name="xnp", bufs=3))
-        grp_pool = ctx.enter_context(tc.tile_pool(name="grpp", bufs=3))
-        q_pool = ctx.enter_context(tc.tile_pool(name="qp", bufs=6))
-        o_pool = ctx.enter_context(tc.tile_pool(name="op", bufs=8))
+        xn_pool = ctx.enter_context(tc.tile_pool(name="xnp", bufs=2))
+        grp_pool = ctx.enter_context(tc.tile_pool(name="grpp", bufs=4))
+        q_pool = ctx.enter_context(tc.tile_pool(name="qp", bufs=8))
+        o_pool = ctx.enter_context(tc.tile_pool(name="op", bufs=6))
         junk_pool = ctx.enter_context(tc.tile_pool(name="junkp", bufs=2))
-        psum = ctx.enter_context(tc.psum_pool(name="ps", bufs=8))
+        psum = ctx.enter_context(tc.psum_pool(name="ps", bufs=1))
+
+        def bank(i, shape, dtype, name):
+            return psum.tile(shape, dtype, name=name, tag="b%d" % (i % 8))
+
+        bias_bf = keep.tile([P, OB], BF16, name="bias_bf")
+        nc.scalar.dma_start(out=bias_bf[:], in_=b_v)
+        xs = [[keep.tile([P, J, PX], BF16, name="x%d%d" % (g, n)) for n in range(NB)] for g in range(G)]
+        for g in range(G):
+            for n, p0, w in PIECES[g]:
+                nc.sync.dma_start(out=xs[g][n][:, :, p0 : p0 + w], in_=x_v[g, n][:, :, p0 : p0 + w])
+        w_sb = keep.tile([P, OB, CH], BF16, name="w_sb")
+        for a in range(OB // 2):
+            nc.sync.dma_start(out=w_sb[:, 2 * a : 2 * a + 2, :], in_=w_v[:, 2 * a : 2 * a + 2, :])
 
         one = keep.tile([P, 1], F32, name="one")
         nc.vector.memset(one[:], 1.0)
         warm = keep.tile([P, 1], F32, name="warm")
         nc.scalar.activation(out=warm[:], in_=one[:], func=ACT.Sqrt)
-        bz = keep.tile([P, P], BF16, name="bz")
-        nc.vector.memset(bz[:], 0.0)
-        ident_b = keep.tile([P, P], BF16, name="ident_b")
-        make_identity(nc, ident_b[:])
         ident_f = keep.tile([P, P], F32, name="ident_f")
         make_identity(nc, ident_f[:])
-
-        nc.scalar.dma_start(out=bz[0:OB, :], in_=bias.rearrange("(r c) -> r c", c=P))
-        xs = [[keep.tile([P, J, PX], BF16, name="x%d%d" % (g, n)) for n in range(NB)] for g in range(G)]
-        for g in range(G):
-            for n in range(NB):
-                if g == 0 and n == 0:
-                    nc.sync.dma_start(out=xs[g][n][:, 0:2, :], in_=x_v[g, n][:, 0:2, :])
-                    nc.sync.dma_start(out=xs[g][n][:, 2:4, :], in_=x_v[g, n][:, 2:4, :])
-                else:
-                    nc.sync.dma_start(out=xs[g][n][:], in_=x_v[g, n])
-        w_sb = [keep.tile([P, 2, CH], BF16, name="w%d" % a) for a in range(OB // 2)]
-        for a in range(OB // 2):
-            nc.sync.dma_start(out=w_sb[a][:], in_=w_v[:, 2 * a : 2 * a + 2, :])
-
-        bt = psum.tile([P, P], BF16, name="bt", tag="bank")
-        nc.tensor.transpose(bt[:], bz[:], ident_b[:])
+        ident_s = keep.tile([P, P], BF16, name="ident_s")
+        nc.vector.tensor_scalar(out=ident_s[:], in0=ident_f[:], scalar1=1.0 / COUNT, scalar2=None, op0=ALU.mult)
+        xT = [keep.tile([P, 4, 2 * XT_PITCH], BF16, name="xT%d" % i) for i in range(N_XT)]
+        for t in xT:
+            nc.vector.memset(t[:, :, 2 * P : 2 * P + 4], 1.0 / COUNT)
         bias_sb = keep.tile([P, OB], F32, name="bias_sb")
-        nc.vector.tensor_copy(out=bias_sb[:], in_=bt[:, 0:OB])
 
         mv = keep.tile([P, G * J, 2], F32, name="mv")
         rstd = keep.tile([P, G * J], F32, name="rstd")
-        for g in range(G):
-            st = keep.tile([P, 2, 2 * NB, 6], F32, name="st%d" % g)
-            negs = keep.tile([P, 2], F32, name="negs%d" % g)
-            acc = keep.tile([P, 2, NB], F32, name="acc%d" % g)
-            sx_ps = [psum.tile([P, PT], F32, name="sx%d%d" % (g, jj), tag="bank") for jj in range(2)]
-            nc.vector.tensor_scalar(
-                out=negs[:], in0=xs[g][0][:, 2:4, 0], scalar1=-1.0, scalar2=None, op0=ALU.mult
-            )
-            for n in range(NB):
-                for j in range(2):
-                    for h in range(2):
-                        nc.vector.bn_stats(
-                            out=st[:, j, 2 * n + h, :], in_=xs[g][n][:, j, PT * h : PT * h + PT]
-                        )
-                for jj in range(2):
-                    junk = junk_pool.tile([P, PX], BF16, name="junk", tag="junk")
-                    nc.scalar.activation(
-                        out=junk[:],
-                        in_=xs[g][n][:, 2 + jj, :],
-                        func=ACT.Square,
-                        bias=negs[:, jj : jj + 1],
-                        scale=1.0,
-                        accum_out=acc[:, jj, n : n + 1],
-                    )
-                    for h in range(2):
-                        nc.tensor.matmul(
-                            sx_ps[jj][:],
-                            lhsT=ident_b[:],
-                            rhs=xs[g][n][:, 2 + jj, PT * h : PT * h + PT],
-                            start=(n == 0 and h == 0),
-                            stop=(n == NB - 1 and h == 1),
-                        )
-            for j in range(2):
-                nc.vector.bn_aggr(out=mv[:, J * g + j, :], in_=st[:, j].rearrange("p a b -> p (a b)"))
-            sx = keep.tile([P, 2], F32, name="sxs%d" % g)
+        ex2 = keep.tile([P, G, J], F32, name="ex2")
+        m2 = keep.tile([P, G, J], F32, name="m2")
+        ve = keep.tile([P, G, J], F32, name="ve")
+        sd = [keep.tile([P, J], F32, name="sd%d" % g) for g in range(G)]
+        junkf = keep.tile([P, P], F32, name="junkf")
+        st = [keep.tile([P, 2, 2 * NB, 6], F32, name="st%d" % g) for g in range(G)]
+        acc = keep.tile([P, len(PIECES[1])], F32, name="acc")
+        gram = [[bank(2 * g + jj, [P, PT], F32, "gram%d%d" % (g, jj)) for jj in range(2)] for g in range(G)]
+        sx_ps = bank(4, [P, PT], F32, "sx_ps")
+        counters = {"t": 0, "m": 0}
+        moved = {}
+
+        def stats_piece(g, k):
+            n, p0, w = PIECES[g][k]
+            for j in BN_J[g]:
+                for h in range(p0 // PT, (p0 + w) // PT):
+                    nc.vector.bn_stats(out=st[g][:, j, 2 * n + h, :], in_=xs[g][n][:, j, PT * h : PT * h + PT])
+            nb = w // (2 * P)
+            xw = xs[g][n][:].bitcast(F32)
             for jj in range(2):
-                nc.vector.tensor_reduce(out=sx[:, jj : jj + 1], in_=sx_ps[jj][:], op=ALU.add, axis=AX.X)
-            ssq = keep.tile([P, 2], F32, name="ssq%d" % g)
-            nc.vector.tensor_reduce(out=ssq[:], in_=acc[:], op=ALU.add, axis=AX.X)
-            mean_s = mv[:, J * g + 2 : J * g + 4, 0]
-            nc.vector.tensor_scalar(out=mean_s, in0=sx[:], scalar1=1.0 / COUNT, scalar2=None, op0=ALU.mult)
-            dd = keep.tile([P, 2], F32, name="dd%d" % g)
-            nc.vector.tensor_tensor(out=dd[:], in0=mean_s, in1=negs[:], op=ALU.add)
-            d2 = keep.tile([P, 2], F32, name="d2%d" % g)
-            nc.vector.tensor_tensor(out=d2[:], in0=dd[:], in1=dd[:], op=ALU.mult)
-            nc.vector.scalar_tensor_tensor(
-                out=mv[:, J * g + 2 : J * g + 4, 1],
-                in0=ssq[:],
-                scalar=1.0 / COUNT,
-                in1=d2[:],
-                op0=ALU.mult,
-                op1=ALU.subtract,
+                t = counters["t"]
+                counters["t"] = t + 1
+                tp = bank(T_BANKS[t % len(T_BANKS)], [P, 4, P], F32, "tp")
+                for b in range(nb):
+                    nc.tensor.transpose(
+                        tp[:, b, :], xw[:, 2 + jj, p0 // 2 + P * b : p0 // 2 + P * b + P], ident_f[:]
+                    )
+                xt = xT[t % N_XT]
+                nc.scalar.copy(out=xt[:].bitcast(F32)[:, 0:nb, 0:P], in_=tp[:, 0:nb, :])
+                moved[(g, k, jj)] = xt
+            if g == 1:
+                junk = junk_pool.tile([P, PX], BF16, name="junk", tag="junk")
+                nc.scalar.activation(
+                    out=junk[:, 0:w],
+                    in_=xs[g][n][:, 1, p0 : p0 + w],
+                    func=ACT.Square,
+                    scale=1.0 / 64.0,
+                    accum_out=acc[:, k : k + 1],
+                )
+                for b in range(w // P):
+                    nc.tensor.matmul(
+                        sx_ps[:, 0:P],
+                        lhsT=ident_s[:],
+                        rhs=xs[g][n][:, 1, p0 + P * b : p0 + P * b + P],
+                        start=(k == 0 and b == 0),
+                        stop=(k == len(PIECES[g]) - 1 and b == w // P - 1),
+                    )
+
+        def gram_piece(g, k):
+            nb = PIECES[g][k][2] // (2 * P)
+            for jj in range(2):
+                halves = moved[(g, k, jj)][:].rearrange("p b (c e) -> p b e c", e=2)
+                for b in range(nb):
+                    for e in range(2):
+                        nc.tensor.matmul(
+                            gram[g][jj][:, 0 : P + 2],
+                            lhsT=halves[:, b, e, 0:P],
+                            rhs=halves[:, b, e, 0 : P + 2],
+                            start=(k == 0 and b == 0 and e == 0),
+                            stop=(k == len(PIECES[g]) - 1 and b == nb - 1 and e == 1),
+                        )
+
+        def chain_a(g):
+            for j in BN_J[g]:
+                nc.vector.bn_aggr(out=mv[:, J * g + j, :], in_=st[g][:, j].rearrange("p a b -> p (a b)"))
+            lo = len(BN_J[g])
+            if g == 1:
+                nc.vector.tensor_reduce(out=ex2[:, g, 1:2], in_=acc[:], op=ALU.add, axis=AX.X)
+                nc.vector.tensor_reduce(out=mv[:, J * g + 1, 0:1], in_=sx_ps[:, 0:P], op=ALU.add, axis=AX.X)
+            for jj in range(2):
+                nc.vector.scalar_tensor_tensor(
+                    out=junkf[:],
+                    in0=gram[g][jj][:, 0:P],
+                    scalar=1.0 / COUNT,
+                    in1=ident_f[:],
+                    op0=ALU.mult,
+                    op1=ALU.mult,
+                    accum_out=ex2[:, g, 2 + jj : 3 + jj],
+                )
+                nc.vector.tensor_copy(out=mv[:, J * g + 2 + jj, 0:1], in_=gram[g][jj][:, P : P + 1])
+            mean_g = mv[:, J * g + lo : J * g + J, 0]
+            nc.vector.tensor_tensor(out=m2[:, g, lo:J], in0=mean_g, in1=mean_g, op=ALU.mult)
+            nc.vector.tensor_tensor(
+                out=mv[:, J * g + lo : J * g + J, 1], in0=ex2[:, g, lo:J], in1=m2[:, g, lo:J], op=ALU.subtract
             )
-            ve = keep.tile([P, J], F32, name="ve%d" % g)
             nc.vector.tensor_scalar(
-                out=ve[:], in0=mv[:, J * g : J * g + J, 1], scalar1=EPS, scalar2=None, op0=ALU.add
+                out=ve[:, g, :], in0=mv[:, J * g : J * g + J, 1], scalar1=EPS, scalar2=None, op0=ALU.add
             )
-            sd = keep.tile([P, J], F32, name="sd%d" % g)
-            nc.scalar.activation(out=sd[:], in_=ve[:], func=ACT.Sqrt)
-            nc.vector.reciprocal(out=rstd[:, J * g : J * g + J], in_=sd[:])
+
+        def chain_s(g):
+            nc.scalar.activation(out=sd[g][:], in_=ve[:, g, :], func=ACT.Sqrt)
+
+        def chain_b(g):
+            nc.vector.reciprocal(out=rstd[:, J * g : J * g + J], in_=sd[g][:])
 
         wg = [keep.tile([P, CH * J], BF16, name="wg%d" % g, align_bytes=64) for g in range(G)]
         wq = [keep.tile([P, CH], U32, name="wq%d" % g, align_bytes=64) for g in range(G)]
         wsc = [keep.tile([P, CH], U8, name="wsc%d" % g, align_bytes=64) for g in range(G)]
-        for a in range(OB // 2):
-            words = w_sb[a][:].bitcast(F32).rearrange("p l (g v u) -> p l g u v", g=G, u=2)
-            for g in range(G):
-                wt = psum.tile([P, 2, 2, P], F32, name="wt", tag="bank")
+        words = w_sb[:].bitcast(F32).rearrange("p ob (g v u) -> p ob g u v", g=G, u=2)
+
+        def w_move(a, gs):
+            for g in gs:
+                wt = bank(WT_BANKS[2 * a + g], [P, 2, 2, P], F32, "wt")
                 for l in range(2):
                     for u in range(2):
-                        nc.tensor.transpose(wt[:, l, u, :], words[:, l, g, u, :], ident_f[:])
+                        nc.tensor.transpose(wt[:, l, u, :], words[:, 2 * a + l, g, u, :], ident_f[:])
                 dst = wg[g][:].bitcast(F32).rearrange("p (o u) -> p o u", u=2)[:, 256 * a : 256 * a + 256, :]
                 nc.scalar.copy(
                     out=dst.rearrange("p (l o) u -> p l o u", l=2),
                     in_=wt[:].rearrange("p l u o -> p l o u"),
                 )
-            for g in range(G):
+
+        def w_quant(a, gs):
+            for g in gs:
                 nc.vector.quantize_mx(
                     out=wq[g][:, 256 * a : 256 * a + 256].bitcast(FP8X4),
                     scales=wsc[g][:, 256 * a : 256 * a + 256],
                     in_=wg[g][:, 1024 * a : 1024 * a + 1024],
                 )
 
-        for pt in range(NB * PX // PT):
-            n, h = pt // 2, pt % 2
-            xq, xsc = [], []
-            for g in range(G):
-                xn = xn_pool.tile([P, J, PT], BF16, name="xn", tag="xn")
-                for j in range(J):
-                    nc.vector.tensor_scalar(
-                        out=xn[:, j, :],
-                        in0=xs[g][n][:, j, PT * h : PT * h + PT],
-                        scalar1=mv[:, J * g + j, 0:1],
-                        scalar2=rstd[:, J * g + j : J * g + j + 1],
-                        op0=ALU.subtract,
-                        op1=ALU.mult,
-                    )
-                grp = grp_pool.tile([P, PT, J], BF16, name="grp", tag="grp", align_bytes=64)
-                nc.vector.tensor_copy(
-                    out=grp[:].rearrange("p (c i) t -> p c t i", i=4),
-                    in_=xn[:].rearrange("p t (c i) -> p c t i", i=4),
+        held = {}
+
+        def norm(g, n, p0, w):
+            if ("xn", g, n) not in held:
+                held[("xn", g, n)] = xn_pool.tile([P, J, PX], BF16, name="xn%d" % g, tag="xn%d" % g)
+            xn = held[("xn", g, n)]
+            for j in range(J):
+                nc.vector.tensor_scalar(
+                    out=xn[:, j, p0 : p0 + w],
+                    in0=xs[g][n][:, j, p0 : p0 + w],
+                    scalar1=mv[:, J * g + j, 0:1],
+                    scalar2=rstd[:, J * g + j : J * g + j + 1],
+                    op0=ALU.subtract,
+                    op1=ALU.mult,
                 )
-                q = q_pool.tile([P, PT], U32, name="xq", tag="xq", align_bytes=64)
-                s = q_pool.tile([P, PT], U8, name="xsc", tag="xsc", align_bytes=64)
-                nc.vector.quantize_mx(
-                    out=q[:].bitcast(FP8X4), scales=s[:], in_=grp[:].rearrange("p w t -> p (w t)")
-                )
-                xq.append(q)
-                xsc.append(s)
-            for ob in range(OB):
-                acc_ps = psum.tile([P, PT], F32, name="mm", tag="bank")
+
+        def regroup(g, u):
+            n, h = divmod(u, 2)
+            grp = grp_pool.tile([P, PT, J], BF16, name="grp", tag="grp", align_bytes=64)
+            nc.vector.tensor_copy(
+                out=grp[:].rearrange("p (c i) t -> p c t i", i=4),
+                in_=held[("xn", g, n)][:, :, PT * h : PT * h + PT].rearrange("p t (c i) -> p c t i", i=4),
+            )
+            held[("grp", g, u)] = grp
+
+        def quant(g, u):
+            q = q_pool.tile([P, PT], U32, name="xq", tag="xq", align_bytes=64)
+            sc = q_pool.tile([P, PT], U8, name="xsc", tag="xsc", align_bytes=64)
+            nc.vector.quantize_mx(
+                out=q[:].bitcast(FP8X4), scales=sc[:], in_=held[("grp", g, u)][:].rearrange("p w t -> p (w t)")
+            )
+            held[("q", g, u)] = (q, sc)
+
+        def multiply(u, a):
+            n, h = divmod(u, 2)
+            ot = o_pool.tile([P, 2, PT], F32, name="ot", tag="ot")
+            for l in range(2):
+                ob = 2 * a + l
+                m = counters["m"]
+                counters["m"] = m + 1
+                acc_ps = bank(m + 2, [P, PT], F32, "mm")
                 for g in range(G):
+                    q, sc = held[("q", g, u)]
                     nc.tensor.matmul_mx(
                         out=acc_ps[:],
                         lhsT=wq[g][:, P * ob : P * ob + P].bitcast(FP8X4),
                         lhsT_scale=wsc[g][:, P * ob : P * ob + P],
-                        rhs=xq[g][:].bitcast(FP8X4),
-                        rhs_scale=xsc[g][:],
+                        rhs=q[:].bitcast(FP8X4),
+                        rhs_scale=sc[:],
                         start=(g == 0),
                         stop=(g == G - 1),
                     )
-                ot = o_pool.tile([P, PT], F32, name="ot", tag="ot")
-                if ob in V_E:
+                if u == NU - 1 and l == 1:
                     nc.vector.tensor_scalar(
-                        out=ot[:], in0=acc_ps[:], scalar1=bias_sb[:, ob : ob + 1], scalar2=None, op0=ALU.add
+                        out=ot[:, l, :], in0=acc_ps[:], scalar1=bias_sb[:, ob : ob + 1], scalar2=None, op0=ALU.add
                     )
                 else:
                     nc.scalar.activation(
-                        out=ot[:], in_=acc_ps[:], func=ACT.Identity, bias=bias_sb[:, ob : ob + 1], scale=1.0
+                        out=ot[:, l, :], in_=acc_ps[:], func=ACT.Identity, bias=bias_sb[:, ob : ob + 1], scale=1.0
                     )
-                nc.sync.dma_start(out=out_v[n, ob][:, PT * h : PT * h + PT], in_=ot[:])
+            nc.sync.dma_start(out=out_v[n][:, 2 * a : 2 * a + 2, PT * h : PT * h + PT], in_=ot[:])
+
+        order = [(g, k) for g in range(G) for k in range(len(PIECES[g]))]
+        for i, (g, k) in enumerate(order):
+            stats_piece(g, k)
+            if i > 0:
+                gram_piece(order[i - 1][0], order[i - 1][1])
+            if (g, k) == (1, 0):
+                chain_a(0)
+            if (g, k) == (1, 1):
+                chain_s(0)
+                chain_b(0)
+                nc.vector.tensor_copy(out=bias_sb[:], in_=bias_bf[:])
+                norm(0, 0, 0, PX)
+            if (g, k) == (1, 2):
+                regroup(0, 0)
+        gram_piece(order[-1][0], order[-1][1])
+        quant(0, 0)
+        chain_a(1)
+        w_move(0, (0,))
+        chain_s(1)
+        w_move(0, (1,))
+        for a in range(1, OB // 2):
+            w_move(a, (0, 1))
+        chain_b(1)
+        norm(1, 0, 0, PT)
+        w_quant(0, (0, 1))
+        regroup(1, 0)
+        w_quant(1, (0,))
+        quant(1, 0)
+        multiply(0, 0)
+        w_quant(1, (1,))
+        multiply(0, 1)
+        w_quant(2, (0, 1))
+        multiply(0, 2)
+        w_quant(3, (0, 1))
+        multiply(0, 3)
+        norm(1, 0, PT, PT)
+        for u in range(1, NU):
+            n, h = divmod(u, 2)
+            regroup(0, u)
+            regroup(1, u)
+            quant(0, u)
+            quant(1, u)
+            for a in range(OB // 2):
+                multiply(u, a)
+            if h == 1 and n + 1 < NB:
+                norm(0, n + 1, 0, PX)
+                norm(1, n + 1, 0, PX)

@@ -28,7 +28,7 @@ FLOPS = 2 * CH * CH * NB * PX
 XT_PITCH = 136
 N_XT = 4
 PIECES = (
-    ((0, 0, 512), (0, 512, 512), (1, 0, 1024), (2, 0, 1024), (3, 0, 1024)),
+    ((0, 0, 1024), (1, 0, 1024), (2, 0, 1024), (3, 0, 1024)),
     ((0, 0, 1024), (1, 0, 1024), (2, 0, 1024), (3, 0, 512), (3, 512, 512)),
 )
 BN_J = ((0, 1), (0,))
@@ -60,8 +60,12 @@ def tile_caps_bn_t_kernel(tc, x, weight, bias, out):
         nc.scalar.dma_start(out=bias_bf[:], in_=b_v)
         xs = [[keep.tile([P, J, PX], BF16, name="x%d%d" % (g, n)) for n in range(NB)] for g in range(G)]
         for g in range(G):
-            for n, p0, w in PIECES[g]:
-                nc.sync.dma_start(out=xs[g][n][:, :, p0 : p0 + w], in_=x_v[g, n][:, :, p0 : p0 + w])
+            for k, (n, p0, w) in enumerate(PIECES[g]):
+                cuts = ((0, 2), (2, 4)) if (g, k) == (0, 0) else ((0, 4),)
+                for j0, j1 in cuts:
+                    nc.sync.dma_start(
+                        out=xs[g][n][:, j0:j1, p0 : p0 + w], in_=x_v[g, n][:, j0:j1, p0 : p0 + w]
+                    )
         w_sb = keep.tile([P, OB, CH], BF16, name="w_sb")
         for a in range(OB // 2):
             nc.sync.dma_start(out=w_sb[:, 2 * a : 2 * a + 2, :], in_=w_v[:, 2 * a : 2 * a + 2, :])
@@ -143,9 +147,15 @@ def tile_caps_bn_t_kernel(tc, x, weight, bias, out):
                             stop=(k == len(PIECES[g]) - 1 and b == nb - 1 and e == 1),
                         )
 
-        def chain_a(g):
+        def chain_bn(g):
+            lo = len(BN_J[g])
             for j in BN_J[g]:
                 nc.vector.bn_aggr(out=mv[:, J * g + j, :], in_=st[g][:, j].rearrange("p a b -> p (a b)"))
+            nc.vector.tensor_scalar(
+                out=ve[:, g, 0:lo], in0=mv[:, J * g : J * g + lo, 1], scalar1=EPS, scalar2=None, op0=ALU.add
+            )
+
+        def chain_a(g):
             lo = len(BN_J[g])
             if g == 1:
                 nc.vector.tensor_reduce(out=ex2[:, g, 1:2], in_=acc[:], op=ALU.add, axis=AX.X)
@@ -163,11 +173,13 @@ def tile_caps_bn_t_kernel(tc, x, weight, bias, out):
                 nc.vector.tensor_copy(out=mv[:, J * g + 2 + jj, 0:1], in_=gram[g][jj][:, P : P + 1])
             mean_g = mv[:, J * g + lo : J * g + J, 0]
             nc.vector.tensor_tensor(out=m2[:, g, lo:J], in0=mean_g, in1=mean_g, op=ALU.mult)
-            nc.vector.tensor_tensor(
-                out=mv[:, J * g + lo : J * g + J, 1], in0=ex2[:, g, lo:J], in1=m2[:, g, lo:J], op=ALU.subtract
-            )
-            nc.vector.tensor_scalar(
-                out=ve[:, g, :], in0=mv[:, J * g : J * g + J, 1], scalar1=EPS, scalar2=None, op0=ALU.add
+            nc.vector.scalar_tensor_tensor(
+                out=ve[:, g, lo:J],
+                in0=ex2[:, g, lo:J],
+                scalar=EPS,
+                in1=m2[:, g, lo:J],
+                op0=ALU.add,
+                op1=ALU.subtract,
             )
 
         def chain_s(g):
@@ -203,14 +215,14 @@ def tile_caps_bn_t_kernel(tc, x, weight, bias, out):
 
         held = {}
 
-        def norm(g, n, p0, w):
-            if ("xn", g, n) not in held:
-                held[("xn", g, n)] = xn_pool.tile([P, J, PX], BF16, name="xn%d" % g, tag="xn%d" % g)
-            xn = held[("xn", g, n)]
+        def norm(g, u):
+            n, h = divmod(u, 2)
+            xn = xn_pool.tile([P, J, PT], BF16, name="xn%d" % g, tag="xn%d" % g)
+            held[("xn", g, u)] = xn
             for j in range(J):
                 nc.vector.tensor_scalar(
-                    out=xn[:, j, p0 : p0 + w],
-                    in0=xs[g][n][:, j, p0 : p0 + w],
+                    out=xn[:, j, :],
+                    in0=xs[g][n][:, j, PT * h : PT * h + PT],
                     scalar1=mv[:, J * g + j, 0:1],
                     scalar2=rstd[:, J * g + j : J * g + j + 1],
                     op0=ALU.subtract,
@@ -218,11 +230,10 @@ def tile_caps_bn_t_kernel(tc, x, weight, bias, out):
                 )
 
         def regroup(g, u):
-            n, h = divmod(u, 2)
             grp = grp_pool.tile([P, PT, J], BF16, name="grp", tag="grp", align_bytes=64)
             nc.vector.tensor_copy(
                 out=grp[:].rearrange("p (c i) t -> p c t i", i=4),
-                in_=held[("xn", g, n)][:, :, PT * h : PT * h + PT].rearrange("p t (c i) -> p c t i", i=4),
+                in_=held[("xn", g, u)][:].rearrange("p t (c i) -> p c t i", i=4),
             )
             held[("grp", g, u)] = grp
 
@@ -234,34 +245,49 @@ def tile_caps_bn_t_kernel(tc, x, weight, bias, out):
             )
             held[("q", g, u)] = (q, sc)
 
-        def multiply(u, a):
+        def passes(u, ob, acc_ps, gs):
+            for g in gs:
+                q, sc = held[("q", g, u)]
+                nc.tensor.matmul_mx(
+                    out=acc_ps[:],
+                    lhsT=wq[g][:, P * ob : P * ob + P].bitcast(FP8X4),
+                    lhsT_scale=wsc[g][:, P * ob : P * ob + P],
+                    rhs=q[:].bitcast(FP8X4),
+                    rhs_scale=sc[:],
+                    start=(g == 0),
+                    stop=(g == G - 1),
+                )
+
+        def new_bank():
+            m = counters["m"]
+            counters["m"] = m + 1
+            return bank(m + 2, [P, PT], F32, "mm")
+
+        def leave(u, a, banks):
             n, h = divmod(u, 2)
             ot = o_pool.tile([P, 2, PT], F32, name="ot", tag="ot")
             for l in range(2):
                 ob = 2 * a + l
-                m = counters["m"]
-                counters["m"] = m + 1
-                acc_ps = bank(m + 2, [P, PT], F32, "mm")
-                for g in range(G):
-                    q, sc = held[("q", g, u)]
-                    nc.tensor.matmul_mx(
-                        out=acc_ps[:],
-                        lhsT=wq[g][:, P * ob : P * ob + P].bitcast(FP8X4),
-                        lhsT_scale=wsc[g][:, P * ob : P * ob + P],
-                        rhs=q[:].bitcast(FP8X4),
-                        rhs_scale=sc[:],
-                        start=(g == 0),
-                        stop=(g == G - 1),
-                    )
                 if u == NU - 1 and l == 1:
                     nc.vector.tensor_scalar(
-                        out=ot[:, l, :], in0=acc_ps[:], scalar1=bias_sb[:, ob : ob + 1], scalar2=None, op0=ALU.add
+                        out=ot[:, l, :], in0=banks[l][:], scalar1=bias_sb[:, ob : ob + 1], scalar2=None, op0=ALU.add
                     )
                 else:
                     nc.scalar.activation(
-                        out=ot[:, l, :], in_=acc_ps[:], func=ACT.Identity, bias=bias_sb[:, ob : ob + 1], scale=1.0
+                        out=ot[:, l, :], in_=banks[l][:], func=ACT.Identity, bias=bias_sb[:, ob : ob + 1], scale=1.0
                     )
-            nc.sync.dma_start(out=out_v[n][:, 2 * a : 2 * a + 2, PT * h : PT * h + PT], in_=ot[:])
+                if u == 0 and a == 0:
+                    nc.sync.dma_start(out=out_v[n][:, ob : ob + 1, PT * h : PT * h + PT], in_=ot[:, l : l + 1, :])
+            if not (u == 0 and a == 0):
+                nc.sync.dma_start(out=out_v[n][:, 2 * a : 2 * a + 2, PT * h : PT * h + PT], in_=ot[:])
+
+        def multiply(u, a):
+            banks = []
+            for l in range(2):
+                acc_ps = new_bank()
+                passes(u, 2 * a + l, acc_ps, (0, 1))
+                banks.append(acc_ps)
+            leave(u, a, banks)
 
         order = [(g, k) for g in range(G) for k in range(len(PIECES[g]))]
         for i, (g, k) in enumerate(order):
@@ -269,15 +295,17 @@ def tile_caps_bn_t_kernel(tc, x, weight, bias, out):
             if i > 0:
                 gram_piece(order[i - 1][0], order[i - 1][1])
             if (g, k) == (1, 0):
+                chain_bn(0)
                 chain_a(0)
             if (g, k) == (1, 1):
                 chain_s(0)
                 chain_b(0)
                 nc.vector.tensor_copy(out=bias_sb[:], in_=bias_bf[:])
-                norm(0, 0, 0, PX)
+                norm(0, 0)
             if (g, k) == (1, 2):
                 regroup(0, 0)
         gram_piece(order[-1][0], order[-1][1])
+        chain_bn(1)
         quant(0, 0)
         chain_a(1)
         w_move(0, (0,))
@@ -286,7 +314,7 @@ def tile_caps_bn_t_kernel(tc, x, weight, bias, out):
         for a in range(1, OB // 2):
             w_move(a, (0, 1))
         chain_b(1)
-        norm(1, 0, 0, PT)
+        norm(1, 0)
         w_quant(0, (0, 1))
         regroup(1, 0)
         w_quant(1, (0,))
@@ -298,15 +326,21 @@ def tile_caps_bn_t_kernel(tc, x, weight, bias, out):
         multiply(0, 2)
         w_quant(3, (0, 1))
         multiply(0, 3)
-        norm(1, 0, PT, PT)
         for u in range(1, NU):
-            n, h = divmod(u, 2)
+            norm(0, u)
+            norm(1, u)
             regroup(0, u)
             regroup(1, u)
             quant(0, u)
+            if u == NU - 1:
+                last = [new_bank() for ob in range(OB)]
+                for ob in range(OB):
+                    passes(u, ob, last[ob], (0,))
             quant(1, u)
             for a in range(OB // 2):
-                multiply(u, a)
-            if h == 1 and n + 1 < NB:
-                norm(0, n + 1, 0, PX)
-                norm(1, n + 1, 0, PX)
+                if u == NU - 1:
+                    for l in range(2):
+                        passes(u, 2 * a + l, last[2 * a + l], (1,))
+                    leave(u, a, last[2 * a : 2 * a + 2])
+                else:
+                    multiply(u, a)

@@ -28,7 +28,7 @@ FLOPS = 2 * CH * CH * NB * PX
 XT_PITCH = 136
 N_XT = 4
 PIECES = (
-    ((0, 0, 1024), (1, 0, 1024), (2, 0, 1024), (3, 0, 1024)),
+    ((0, 0, 512), (0, 512, 512), (1, 0, 1024), (2, 0, 1024), (3, 0, 1024)),
     ((0, 0, 1024), (1, 0, 1024), (2, 0, 1024), (3, 0, 512), (3, 512, 512)),
 )
 BN_J = ((0, 1), (0,))
@@ -44,7 +44,6 @@ def tile_caps_bn_t_kernel(tc, x, weight, bias, out):
     out_v = out.rearrange("n (p ob) h w -> n p ob (h w)", ob=OB)
 
     with ExitStack() as ctx:
-        ctx.enter_context(tc.manual_schedule())
         keep = ctx.enter_context(tc.tile_pool(name="keep", bufs=1))
         xn_pool = ctx.enter_context(tc.tile_pool(name="xnp", bufs=2))
         grp_pool = ctx.enter_context(tc.tile_pool(name="grpp", bufs=4))
@@ -60,12 +59,8 @@ def tile_caps_bn_t_kernel(tc, x, weight, bias, out):
         nc.scalar.dma_start(out=bias_bf[:], in_=b_v)
         xs = [[keep.tile([P, J, PX], BF16, name="x%d%d" % (g, n)) for n in range(NB)] for g in range(G)]
         for g in range(G):
-            for k, (n, p0, w) in enumerate(PIECES[g]):
-                cuts = ((0, 2), (2, 4)) if (g, k) == (0, 0) else ((0, 4),)
-                for j0, j1 in cuts:
-                    nc.sync.dma_start(
-                        out=xs[g][n][:, j0:j1, p0 : p0 + w], in_=x_v[g, n][:, j0:j1, p0 : p0 + w]
-                    )
+            for n, p0, w in PIECES[g]:
+                nc.sync.dma_start(out=xs[g][n][:, :, p0 : p0 + w], in_=x_v[g, n][:, :, p0 : p0 + w])
         w_sb = keep.tile([P, OB, CH], BF16, name="w_sb")
         for a in range(OB // 2):
             nc.sync.dma_start(out=w_sb[:, 2 * a : 2 * a + 2, :], in_=w_v[:, 2 * a : 2 * a + 2, :])
@@ -147,15 +142,9 @@ def tile_caps_bn_t_kernel(tc, x, weight, bias, out):
                             stop=(k == len(PIECES[g]) - 1 and b == nb - 1 and e == 1),
                         )
 
-        def chain_bn(g):
-            lo = len(BN_J[g])
+        def chain_a(g):
             for j in BN_J[g]:
                 nc.vector.bn_aggr(out=mv[:, J * g + j, :], in_=st[g][:, j].rearrange("p a b -> p (a b)"))
-            nc.vector.tensor_scalar(
-                out=ve[:, g, 0:lo], in0=mv[:, J * g : J * g + lo, 1], scalar1=EPS, scalar2=None, op0=ALU.add
-            )
-
-        def chain_a(g):
             lo = len(BN_J[g])
             if g == 1:
                 nc.vector.tensor_reduce(out=ex2[:, g, 1:2], in_=acc[:], op=ALU.add, axis=AX.X)
@@ -173,13 +162,11 @@ def tile_caps_bn_t_kernel(tc, x, weight, bias, out):
                 nc.vector.tensor_copy(out=mv[:, J * g + 2 + jj, 0:1], in_=gram[g][jj][:, P : P + 1])
             mean_g = mv[:, J * g + lo : J * g + J, 0]
             nc.vector.tensor_tensor(out=m2[:, g, lo:J], in0=mean_g, in1=mean_g, op=ALU.mult)
-            nc.vector.scalar_tensor_tensor(
-                out=ve[:, g, lo:J],
-                in0=ex2[:, g, lo:J],
-                scalar=EPS,
-                in1=m2[:, g, lo:J],
-                op0=ALU.add,
-                op1=ALU.subtract,
+            nc.vector.tensor_tensor(
+                out=mv[:, J * g + lo : J * g + J, 1], in0=ex2[:, g, lo:J], in1=m2[:, g, lo:J], op=ALU.subtract
+            )
+            nc.vector.tensor_scalar(
+                out=ve[:, g, :], in0=mv[:, J * g : J * g + J, 1], scalar1=EPS, scalar2=None, op0=ALU.add
             )
 
         def chain_s(g):
@@ -215,14 +202,14 @@ def tile_caps_bn_t_kernel(tc, x, weight, bias, out):
 
         held = {}
 
-        def norm(g, u):
-            n, h = divmod(u, 2)
-            xn = xn_pool.tile([P, J, PT], BF16, name="xn%d" % g, tag="xn%d" % g)
-            held[("xn", g, u)] = xn
+        def norm(g, n, p0, w):
+            if ("xn", g, n) not in held:
+                held[("xn", g, n)] = xn_pool.tile([P, J, PX], BF16, name="xn%d" % g, tag="xn%d" % g)
+            xn = held[("xn", g, n)]
             for j in range(J):
                 nc.vector.tensor_scalar(
-                    out=xn[:, j, :],
-                    in0=xs[g][n][:, j, PT * h : PT * h + PT],
+                    out=xn[:, j, p0 : p0 + w],
+                    in0=xs[g][n][:, j, p0 : p0 + w],
                     scalar1=mv[:, J * g + j, 0:1],
                     scalar2=rstd[:, J * g + j : J * g + j + 1],
                     op0=ALU.subtract,
@@ -230,10 +217,11 @@ def tile_caps_bn_t_kernel(tc, x, weight, bias, out):
                 )
 
         def regroup(g, u):
+            n, h = divmod(u, 2)
             grp = grp_pool.tile([P, PT, J], BF16, name="grp", tag="grp", align_bytes=64)
             nc.vector.tensor_copy(
                 out=grp[:].rearrange("p (c i) t -> p c t i", i=4),
-                in_=held[("xn", g, u)][:].rearrange("p t (c i) -> p c t i", i=4),
+                in_=held[("xn", g, n)][:, :, PT * h : PT * h + PT].rearrange("p t (c i) -> p c t i", i=4),
             )
             held[("grp", g, u)] = grp
 
@@ -245,49 +233,34 @@ def tile_caps_bn_t_kernel(tc, x, weight, bias, out):
             )
             held[("q", g, u)] = (q, sc)
 
-        def passes(u, ob, acc_ps, gs):
-            for g in gs:
-                q, sc = held[("q", g, u)]
-                nc.tensor.matmul_mx(
-                    out=acc_ps[:],
-                    lhsT=wq[g][:, P * ob : P * ob + P].bitcast(FP8X4),
-                    lhsT_scale=wsc[g][:, P * ob : P * ob + P],
-                    rhs=q[:].bitcast(FP8X4),
-                    rhs_scale=sc[:],
-                    start=(g == 0),
-                    stop=(g == G - 1),
-                )
-
-        def new_bank():
-            m = counters["m"]
-            counters["m"] = m + 1
-            return bank(m + 2, [P, PT], F32, "mm")
-
-        def leave(u, a, banks):
+        def multiply(u, a):
             n, h = divmod(u, 2)
             ot = o_pool.tile([P, 2, PT], F32, name="ot", tag="ot")
             for l in range(2):
                 ob = 2 * a + l
+                m = counters["m"]
+                counters["m"] = m + 1
+                acc_ps = bank(m + 2, [P, PT], F32, "mm")
+                for g in range(G):
+                    q, sc = held[("q", g, u)]
+                    nc.tensor.matmul_mx(
+                        out=acc_ps[:],
+                        lhsT=wq[g][:, P * ob : P * ob + P].bitcast(FP8X4),
+                        lhsT_scale=wsc[g][:, P * ob : P * ob + P],
+                        rhs=q[:].bitcast(FP8X4),
+                        rhs_scale=sc[:],
+                        start=(g == 0),
+                        stop=(g == G - 1),
+                    )
                 if u == NU - 1 and l == 1:
                     nc.vector.tensor_scalar(
-                        out=ot[:, l, :], in0=banks[l][:], scalar1=bias_sb[:, ob : ob + 1], scalar2=None, op0=ALU.add
+                        out=ot[:, l, :], in0=acc_ps[:], scalar1=bias_sb[:, ob : ob + 1], scalar2=None, op0=ALU.add
                     )
                 else:
                     nc.scalar.activation(
-                        out=ot[:, l, :], in_=banks[l][:], func=ACT.Identity, bias=bias_sb[:, ob : ob + 1], scale=1.0
+                        out=ot[:, l, :], in_=acc_ps[:], func=ACT.Identity, bias=bias_sb[:, ob : ob + 1], scale=1.0
                     )
-                if u == 0 and a == 0:
-                    nc.sync.dma_start(out=out_v[n][:, ob : ob + 1, PT * h : PT * h + PT], in_=ot[:, l : l + 1, :])
-            if not (u == 0 and a == 0):
-                nc.sync.dma_start(out=out_v[n][:, 2 * a : 2 * a + 2, PT * h : PT * h + PT], in_=ot[:])
-
-        def multiply(u, a):
-            banks = []
-            for l in range(2):
-                acc_ps = new_bank()
-                passes(u, 2 * a + l, acc_ps, (0, 1))
-                banks.append(acc_ps)
-            leave(u, a, banks)
+            nc.sync.dma_start(out=out_v[n][:, 2 * a : 2 * a + 2, PT * h : PT * h + PT], in_=ot[:])
 
         order = [(g, k) for g in range(G) for k in range(len(PIECES[g]))]
         for i, (g, k) in enumerate(order):
@@ -295,17 +268,15 @@ def tile_caps_bn_t_kernel(tc, x, weight, bias, out):
             if i > 0:
                 gram_piece(order[i - 1][0], order[i - 1][1])
             if (g, k) == (1, 0):
-                chain_bn(0)
                 chain_a(0)
             if (g, k) == (1, 1):
                 chain_s(0)
                 chain_b(0)
                 nc.vector.tensor_copy(out=bias_sb[:], in_=bias_bf[:])
-                norm(0, 0)
+                norm(0, 0, 0, PX)
             if (g, k) == (1, 2):
                 regroup(0, 0)
         gram_piece(order[-1][0], order[-1][1])
-        chain_bn(1)
         quant(0, 0)
         chain_a(1)
         w_move(0, (0,))
@@ -314,7 +285,7 @@ def tile_caps_bn_t_kernel(tc, x, weight, bias, out):
         for a in range(1, OB // 2):
             w_move(a, (0, 1))
         chain_b(1)
-        norm(1, 0)
+        norm(1, 0, 0, PT)
         w_quant(0, (0, 1))
         regroup(1, 0)
         w_quant(1, (0,))
@@ -326,21 +297,15 @@ def tile_caps_bn_t_kernel(tc, x, weight, bias, out):
         multiply(0, 2)
         w_quant(3, (0, 1))
         multiply(0, 3)
+        norm(1, 0, PT, PT)
         for u in range(1, NU):
-            norm(0, u)
-            norm(1, u)
+            n, h = divmod(u, 2)
             regroup(0, u)
             regroup(1, u)
             quant(0, u)
-            if u == NU - 1:
-                last = [new_bank() for ob in range(OB)]
-                for ob in range(OB):
-                    passes(u, ob, last[ob], (0,))
             quant(1, u)
             for a in range(OB // 2):
-                if u == NU - 1:
-                    for l in range(2):
-                        passes(u, 2 * a + l, last[2 * a + l], (1,))
-                    leave(u, a, last[2 * a : 2 * a + 2])
-                else:
-                    multiply(u, a)
+                multiply(u, a)
+            if h == 1 and n + 1 < NB:
+                norm(0, n + 1, 0, PX)
+                norm(1, n + 1, 0, PX)

@@ -28,7 +28,7 @@ FLOPS = 2 * CH * CH * NB * PX
 XT_PITCH = 136
 N_XT = 4
 PIECES = (
-    ((0, 0, 512), (0, 512, 512), (1, 0, 1024), (2, 0, 1024), (3, 0, 1024)),
+    ((0, 0, 1024), (1, 0, 1024), (2, 0, 1024), (3, 0, 1024)),
     ((0, 0, 1024), (1, 0, 1024), (2, 0, 1024), (3, 0, 512), (3, 512, 512)),
 )
 BN_J = ((0, 1), (0,))
@@ -44,6 +44,7 @@ def tile_caps_bn_t_kernel(tc, x, weight, bias, out):
     out_v = out.rearrange("n (p ob) h w -> n p ob (h w)", ob=OB)
 
     with ExitStack() as ctx:
+        ctx.enter_context(tc.manual_schedule())
         keep = ctx.enter_context(tc.tile_pool(name="keep", bufs=1))
         xn_pool = ctx.enter_context(tc.tile_pool(name="xnp", bufs=2))
         grp_pool = ctx.enter_context(tc.tile_pool(name="grpp", bufs=4))
@@ -59,8 +60,12 @@ def tile_caps_bn_t_kernel(tc, x, weight, bias, out):
         nc.scalar.dma_start(out=bias_bf[:], in_=b_v)
         xs = [[keep.tile([P, J, PX], BF16, name="x%d%d" % (g, n)) for n in range(NB)] for g in range(G)]
         for g in range(G):
-            for n, p0, w in PIECES[g]:
-                nc.sync.dma_start(out=xs[g][n][:, :, p0 : p0 + w], in_=x_v[g, n][:, :, p0 : p0 + w])
+            for k, (n, p0, w) in enumerate(PIECES[g]):
+                cuts = ((0, 2), (2, 4)) if (g, k) == (0, 0) else ((0, 4),)
+                for j0, j1 in cuts:
+                    nc.sync.dma_start(
+                        out=xs[g][n][:, j0:j1, p0 : p0 + w], in_=x_v[g, n][:, j0:j1, p0 : p0 + w]
+                    )
         w_sb = keep.tile([P, OB, CH], BF16, name="w_sb")
         for a in range(OB // 2):
             nc.sync.dma_start(out=w_sb[:, 2 * a : 2 * a + 2, :], in_=w_v[:, 2 * a : 2 * a + 2, :])
@@ -76,7 +81,6 @@ def tile_caps_bn_t_kernel(tc, x, weight, bias, out):
         xT = [keep.tile([P, 4, 2 * XT_PITCH], BF16, name="xT%d" % i) for i in range(N_XT)]
         for t in xT:
             nc.vector.memset(t[:, :, 2 * P : 2 * P + 4], 1.0 / COUNT)
-        bias_sb = keep.tile([P, OB], F32, name="bias_sb")
 
         mv = keep.tile([P, G * J, 2], F32, name="mv")
         rstd = keep.tile([P, G * J], F32, name="rstd")
@@ -142,9 +146,15 @@ def tile_caps_bn_t_kernel(tc, x, weight, bias, out):
                             stop=(k == len(PIECES[g]) - 1 and b == nb - 1 and e == 1),
                         )
 
-        def chain_a(g):
+        def chain_bn(g):
+            lo = len(BN_J[g])
             for j in BN_J[g]:
                 nc.vector.bn_aggr(out=mv[:, J * g + j, :], in_=st[g][:, j].rearrange("p a b -> p (a b)"))
+            nc.vector.tensor_scalar(
+                out=ve[:, g, 0:lo], in0=mv[:, J * g : J * g + lo, 1], scalar1=EPS, scalar2=None, op0=ALU.add
+            )
+
+        def chain_a(g):
             lo = len(BN_J[g])
             if g == 1:
                 nc.vector.tensor_reduce(out=ex2[:, g, 1:2], in_=acc[:], op=ALU.add, axis=AX.X)
@@ -162,11 +172,13 @@ def tile_caps_bn_t_kernel(tc, x, weight, bias, out):
                 nc.vector.tensor_copy(out=mv[:, J * g + 2 + jj, 0:1], in_=gram[g][jj][:, P : P + 1])
             mean_g = mv[:, J * g + lo : J * g + J, 0]
             nc.vector.tensor_tensor(out=m2[:, g, lo:J], in0=mean_g, in1=mean_g, op=ALU.mult)
-            nc.vector.tensor_tensor(
-                out=mv[:, J * g + lo : J * g + J, 1], in0=ex2[:, g, lo:J], in1=m2[:, g, lo:J], op=ALU.subtract
-            )
-            nc.vector.tensor_scalar(
-                out=ve[:, g, :], in0=mv[:, J * g : J * g + J, 1], scalar1=EPS, scalar2=None, op0=ALU.add
+            nc.vector.scalar_tensor_tensor(
+                out=ve[:, g, lo:J],
+                in0=ex2[:, g, lo:J],
+                scalar=EPS,
+                in1=m2[:, g, lo:J],
+                op0=ALU.add,
+                op1=ALU.subtract,
             )
 
         def chain_s(g):
@@ -175,9 +187,9 @@ def tile_caps_bn_t_kernel(tc, x, weight, bias, out):
         def chain_b(g):
             nc.vector.reciprocal(out=rstd[:, J * g : J * g + J], in_=sd[g][:])
 
-        wg = [keep.tile([P, CH * J], BF16, name="wg%d" % g, align_bytes=64) for g in range(G)]
-        wq = [keep.tile([P, CH], U32, name="wq%d" % g, align_bytes=64) for g in range(G)]
-        wsc = [keep.tile([P, CH], U8, name="wsc%d" % g, align_bytes=64) for g in range(G)]
+        wg = keep.tile([P, OB // 2, G, 4 * 2 * P], BF16, name="wg", align_bytes=64)
+        wq = keep.tile([P, OB // 2, G, 2 * P], U32, name="wq", align_bytes=64)
+        wsc = keep.tile([P, OB // 2, G, 2 * P], U8, name="wsc", align_bytes=64)
         words = w_sb[:].bitcast(F32).rearrange("p ob (g v u) -> p ob g u v", g=G, u=2)
 
         def w_move(a, gs):
@@ -186,19 +198,17 @@ def tile_caps_bn_t_kernel(tc, x, weight, bias, out):
                 for l in range(2):
                     for u in range(2):
                         nc.tensor.transpose(wt[:, l, u, :], words[:, 2 * a + l, g, u, :], ident_f[:])
-                dst = wg[g][:].bitcast(F32).rearrange("p (o u) -> p o u", u=2)[:, 256 * a : 256 * a + 256, :]
                 nc.scalar.copy(
-                    out=dst.rearrange("p (l o) u -> p l o u", l=2),
+                    out=wg[:, a, g, :].bitcast(F32).rearrange("p (l o u) -> p l o u", l=2, u=2),
                     in_=wt[:].rearrange("p l u o -> p l o u"),
                 )
 
-        def w_quant(a, gs):
-            for g in gs:
-                nc.vector.quantize_mx(
-                    out=wq[g][:, 256 * a : 256 * a + 256].bitcast(FP8X4),
-                    scales=wsc[g][:, 256 * a : 256 * a + 256],
-                    in_=wg[g][:, 1024 * a : 1024 * a + 1024],
-                )
+        def w_quant(a):
+            nc.vector.quantize_mx(
+                out=wq[:, a].rearrange("p g c -> p (g c)").bitcast(FP8X4),
+                scales=wsc[:, a].rearrange("p g c -> p (g c)"),
+                in_=wg[:, a].rearrange("p g c -> p (g c)"),
+            )
 
         held = {}
 
@@ -245,8 +255,8 @@ def tile_caps_bn_t_kernel(tc, x, weight, bias, out):
                     q, sc = held[("q", g, u)]
                     nc.tensor.matmul_mx(
                         out=acc_ps[:],
-                        lhsT=wq[g][:, P * ob : P * ob + P].bitcast(FP8X4),
-                        lhsT_scale=wsc[g][:, P * ob : P * ob + P],
+                        lhsT=wq[:, a, g, P * l : P * l + P].bitcast(FP8X4),
+                        lhsT_scale=wsc[:, a, g, P * l : P * l + P],
                         rhs=q[:].bitcast(FP8X4),
                         rhs_scale=sc[:],
                         start=(g == 0),
@@ -254,11 +264,11 @@ def tile_caps_bn_t_kernel(tc, x, weight, bias, out):
                     )
                 if u == NU - 1 and l == 1:
                     nc.vector.tensor_scalar(
-                        out=ot[:, l, :], in0=acc_ps[:], scalar1=bias_sb[:, ob : ob + 1], scalar2=None, op0=ALU.add
+                        out=ot[:, l, :], in0=acc_ps[:], scalar1=bias_bf[:, ob : ob + 1], scalar2=None, op0=ALU.add
                     )
                 else:
                     nc.scalar.activation(
-                        out=ot[:, l, :], in_=acc_ps[:], func=ACT.Identity, bias=bias_sb[:, ob : ob + 1], scale=1.0
+                        out=ot[:, l, :], in_=acc_ps[:], func=ACT.Identity, bias=bias_bf[:, ob : ob + 1], scale=1.0
                     )
             nc.sync.dma_start(out=out_v[n][:, 2 * a : 2 * a + 2, PT * h : PT * h + PT], in_=ot[:])
 
@@ -268,15 +278,16 @@ def tile_caps_bn_t_kernel(tc, x, weight, bias, out):
             if i > 0:
                 gram_piece(order[i - 1][0], order[i - 1][1])
             if (g, k) == (1, 0):
+                chain_bn(0)
                 chain_a(0)
             if (g, k) == (1, 1):
                 chain_s(0)
                 chain_b(0)
-                nc.vector.tensor_copy(out=bias_sb[:], in_=bias_bf[:])
                 norm(0, 0, 0, PX)
             if (g, k) == (1, 2):
                 regroup(0, 0)
         gram_piece(order[-1][0], order[-1][1])
+        chain_bn(1)
         quant(0, 0)
         chain_a(1)
         w_move(0, (0,))
@@ -286,16 +297,15 @@ def tile_caps_bn_t_kernel(tc, x, weight, bias, out):
             w_move(a, (0, 1))
         chain_b(1)
         norm(1, 0, 0, PT)
-        w_quant(0, (0, 1))
+        w_quant(0)
         regroup(1, 0)
-        w_quant(1, (0,))
+        w_quant(1)
         quant(1, 0)
         multiply(0, 0)
-        w_quant(1, (1,))
         multiply(0, 1)
-        w_quant(2, (0, 1))
+        w_quant(2)
         multiply(0, 2)
-        w_quant(3, (0, 1))
+        w_quant(3)
         multiply(0, 3)
         norm(1, 0, PT, PT)
         for u in range(1, NU):

@@ -46,9 +46,9 @@ def tile_caps_bn_t_kernel(tc, x, weight, bias, out):
     with ExitStack() as ctx:
         ctx.enter_context(tc.manual_schedule())
         keep = ctx.enter_context(tc.tile_pool(name="keep", bufs=1))
-        xn_pool = ctx.enter_context(tc.tile_pool(name="xnp", bufs=2))
         grp_pool = ctx.enter_context(tc.tile_pool(name="grpp", bufs=4))
-        q_pool = ctx.enter_context(tc.tile_pool(name="qp", bufs=8))
+        q0_pool = ctx.enter_context(tc.tile_pool(name="q0p", bufs=8))
+        q1_pool = ctx.enter_context(tc.tile_pool(name="q1p", bufs=3))
         o_pool = ctx.enter_context(tc.tile_pool(name="op", bufs=6))
         junk_pool = ctx.enter_context(tc.tile_pool(name="junkp", bufs=2))
         psum = ctx.enter_context(tc.psum_pool(name="ps", bufs=1))
@@ -61,7 +61,7 @@ def tile_caps_bn_t_kernel(tc, x, weight, bias, out):
         xs = [[keep.tile([P, J, PX], BF16, name="x%d%d" % (g, n)) for n in range(NB)] for g in range(G)]
         for g in range(G):
             for k, (n, p0, w) in enumerate(PIECES[g]):
-                cuts = ((0, 2), (2, 4)) if (g, k) == (0, 0) else ((0, 4),)
+                cuts = ((0, 1), (2, 3), (1, 2), (3, 4)) if (g, k) == (0, 0) else ((0, 2), (2, 4))
                 for j0, j1 in cuts:
                     nc.sync.dma_start(
                         out=xs[g][n][:, j0:j1, p0 : p0 + w], in_=x_v[g, n][:, j0:j1, p0 : p0 + w]
@@ -96,11 +96,14 @@ def tile_caps_bn_t_kernel(tc, x, weight, bias, out):
         counters = {"t": 0, "m": 0}
         moved = {}
 
-        def stats_piece(g, k):
+        def bn_piece(g, k):
             n, p0, w = PIECES[g][k]
             for j in BN_J[g]:
                 for h in range(p0 // PT, (p0 + w) // PT):
                     nc.vector.bn_stats(out=st[g][:, j, 2 * n + h, :], in_=xs[g][n][:, j, PT * h : PT * h + PT])
+
+        def turn_piece(g, k):
+            n, p0, w = PIECES[g][k]
             nb = w // (2 * P)
             xw = xs[g][n][:].bitcast(F32)
             for jj in range(2):
@@ -114,23 +117,25 @@ def tile_caps_bn_t_kernel(tc, x, weight, bias, out):
                 xt = xT[t % N_XT]
                 nc.scalar.copy(out=xt[:].bitcast(F32)[:, 0:nb, 0:P], in_=tp[:, 0:nb, :])
                 moved[(g, k, jj)] = xt
-            if g == 1:
-                junk = junk_pool.tile([P, PX], BF16, name="junk", tag="junk")
-                nc.scalar.activation(
-                    out=junk[:, 0:w],
-                    in_=xs[g][n][:, 1, p0 : p0 + w],
-                    func=ACT.Square,
-                    scale=1.0 / 64.0,
-                    accum_out=acc[:, k : k + 1],
+
+        def square_piece(g, k):
+            n, p0, w = PIECES[g][k]
+            junk = junk_pool.tile([P, PX], BF16, name="junk", tag="junk")
+            nc.scalar.activation(
+                out=junk[:, 0:w],
+                in_=xs[g][n][:, 1, p0 : p0 + w],
+                func=ACT.Square,
+                scale=1.0 / 64.0,
+                accum_out=acc[:, k : k + 1],
+            )
+            for b in range(w // P):
+                nc.tensor.matmul(
+                    sx_ps[:, 0:P],
+                    lhsT=ident_s[:],
+                    rhs=xs[g][n][:, 1, p0 + P * b : p0 + P * b + P],
+                    start=(k == 0 and b == 0),
+                    stop=(k == len(PIECES[g]) - 1 and b == w // P - 1),
                 )
-                for b in range(w // P):
-                    nc.tensor.matmul(
-                        sx_ps[:, 0:P],
-                        lhsT=ident_s[:],
-                        rhs=xs[g][n][:, 1, p0 + P * b : p0 + P * b + P],
-                        start=(k == 0 and b == 0),
-                        stop=(k == len(PIECES[g]) - 1 and b == w // P - 1),
-                    )
 
         def gram_piece(g, k):
             nb = PIECES[g][k][2] // (2 * P)
@@ -213,12 +218,9 @@ def tile_caps_bn_t_kernel(tc, x, weight, bias, out):
         held = {}
 
         def norm(g, n, p0, w):
-            if ("xn", g, n) not in held:
-                held[("xn", g, n)] = xn_pool.tile([P, J, PX], BF16, name="xn%d" % g, tag="xn%d" % g)
-            xn = held[("xn", g, n)]
             for j in range(J):
                 nc.vector.tensor_scalar(
-                    out=xn[:, j, p0 : p0 + w],
+                    out=xs[g][n][:, j, p0 : p0 + w],
                     in0=xs[g][n][:, j, p0 : p0 + w],
                     scalar1=mv[:, J * g + j, 0:1],
                     scalar2=rstd[:, J * g + j : J * g + j + 1],
@@ -231,19 +233,20 @@ def tile_caps_bn_t_kernel(tc, x, weight, bias, out):
             grp = grp_pool.tile([P, PT, J], BF16, name="grp", tag="grp", align_bytes=64)
             nc.vector.tensor_copy(
                 out=grp[:].rearrange("p (c i) t -> p c t i", i=4),
-                in_=held[("xn", g, n)][:, :, PT * h : PT * h + PT].rearrange("p t (c i) -> p c t i", i=4),
+                in_=xs[g][n][:, :, PT * h : PT * h + PT].rearrange("p t (c i) -> p c t i", i=4),
             )
             held[("grp", g, u)] = grp
 
         def quant(g, u):
-            q = q_pool.tile([P, PT], U32, name="xq", tag="xq", align_bytes=64)
-            sc = q_pool.tile([P, PT], U8, name="xsc", tag="xsc", align_bytes=64)
+            pool = q0_pool if g == 0 else q1_pool
+            q = pool.tile([P, PT], U32, name="xq", tag="xq", align_bytes=64)
+            sc = pool.tile([P, PT], U8, name="xsc", tag="xsc", align_bytes=64)
             nc.vector.quantize_mx(
                 out=q[:].bitcast(FP8X4), scales=sc[:], in_=held[("grp", g, u)][:].rearrange("p w t -> p (w t)")
             )
             held[("q", g, u)] = (q, sc)
 
-        def multiply(u, a):
+        def multiply(u, a, on_vector=()):
             n, h = divmod(u, 2)
             ot = o_pool.tile([P, 2, PT], F32, name="ot", tag="ot")
             for l in range(2):
@@ -262,7 +265,7 @@ def tile_caps_bn_t_kernel(tc, x, weight, bias, out):
                         start=(g == 0),
                         stop=(g == G - 1),
                     )
-                if u == NU - 1 and l == 1:
+                if l in on_vector:
                     nc.vector.tensor_scalar(
                         out=ot[:, l, :], in0=acc_ps[:], scalar1=bias_bf[:, ob : ob + 1], scalar2=None, op0=ALU.add
                     )
@@ -272,50 +275,76 @@ def tile_caps_bn_t_kernel(tc, x, weight, bias, out):
                     )
             nc.sync.dma_start(out=out_v[n][:, 2 * a : 2 * a + 2, PT * h : PT * h + PT], in_=ot[:])
 
-        order = [(g, k) for g in range(G) for k in range(len(PIECES[g]))]
-        for i, (g, k) in enumerate(order):
-            stats_piece(g, k)
-            if i > 0:
-                gram_piece(order[i - 1][0], order[i - 1][1])
-            if (g, k) == (1, 0):
-                chain_bn(0)
-                chain_a(0)
-            if (g, k) == (1, 1):
-                chain_s(0)
-                chain_b(0)
-                norm(0, 0, 0, PX)
-            if (g, k) == (1, 2):
-                regroup(0, 0)
-        gram_piece(order[-1][0], order[-1][1])
-        chain_bn(1)
+        bn_piece(0, 0)
+        turn_piece(0, 0)
+        for k in range(1, 4):
+            bn_piece(0, k)
+            turn_piece(0, k)
+            gram_piece(0, k - 1)
+        gram_piece(0, 3)
+        chain_bn(0)
+        bn_piece(1, 0)
+        chain_a(0)
+        chain_s(0)
+        turn_piece(1, 0)
+        square_piece(1, 0)
+        chain_b(0)
+        norm(0, 0, 0, PX)
+        bn_piece(1, 1)
+        turn_piece(1, 1)
+        square_piece(1, 1)
+        gram_piece(1, 0)
+        regroup(0, 0)
+        bn_piece(1, 2)
+        turn_piece(1, 2)
+        square_piece(1, 2)
+        gram_piece(1, 1)
         quant(0, 0)
+        regroup(0, 1)
+        bn_piece(1, 3)
+        turn_piece(1, 3)
+        square_piece(1, 3)
+        gram_piece(1, 2)
+        quant(0, 1)
+        bn_piece(1, 4)
+        turn_piece(1, 4)
+        square_piece(1, 4)
+        gram_piece(1, 3)
+        gram_piece(1, 4)
+        chain_bn(1)
         chain_a(1)
-        w_move(0, (0,))
         chain_s(1)
-        w_move(0, (1,))
-        for a in range(1, OB // 2):
-            w_move(a, (0, 1))
+        w_move(0, (0, 1))
         chain_b(1)
         norm(1, 0, 0, PT)
-        w_quant(0)
         regroup(1, 0)
-        w_quant(1)
+        w_quant(0)
+        for a in range(1, OB // 2):
+            w_move(a, (0, 1))
         quant(1, 0)
         multiply(0, 0)
+        w_quant(1)
         multiply(0, 1)
         w_quant(2)
         multiply(0, 2)
         w_quant(3)
         multiply(0, 3)
         norm(1, 0, PT, PT)
+        regroup(1, 1)
+        quant(1, 1)
         for u in range(1, NU):
             n, h = divmod(u, 2)
-            regroup(0, u)
-            regroup(1, u)
-            quant(0, u)
-            quant(1, u)
+            if u + 1 < NU:
+                n1, h1 = divmod(u + 1, 2)
+                if n1 == NB - 1:
+                    norm(0, n1, PT * h1, PT)
+                    norm(1, n1, PT * h1, PT)
+                elif h1 == 0:
+                    norm(0, n1, 0, PX)
+                    norm(1, n1, 0, PX)
+                regroup(0, u + 1)
+                regroup(1, u + 1)
+                quant(0, u + 1)
+                quant(1, u + 1)
             for a in range(OB // 2):
-                multiply(u, a)
-            if h == 1 and n + 1 < NB:
-                norm(0, n + 1, 0, PX)
-                norm(1, n + 1, 0, PX)
+                multiply(u, a, (1,) if u == NU - 1 else ())

@@ -232,8 +232,8 @@ def tile_caps_bn_t_kernel(tc, x, weight, bias, out):
             n, h = divmod(u, 2)
             grp = grp_pool.tile([P, PT, J], BF16, name="grp", tag="grp", align_bytes=64)
             nc.vector.tensor_copy(
-                out=grp[:].rearrange("p (c i) t -> p c t i", i=4),
-                in_=xs[g][n][:, :, PT * h : PT * h + PT].rearrange("p t (c i) -> p c t i", i=4),
+                out=grp[:].rearrange("p (c i) t -> p c t i", i=8),
+                in_=xs[g][n][:, :, PT * h : PT * h + PT].rearrange("p t (c i) -> p c t i", i=8),
             )
             held[("grp", g, u)] = grp
 

from contextlib import ExitStack

import concourse.mybir as mybir
from concourse.masks import make_identity

F32 = mybir.dt.float32
BF16 = mybir.dt.bfloat16
U32 = mybir.dt.uint32
U8 = mybir.dt.uint8
FP8X4 = mybir.dt.float8_e4m3fn_x4
ALU = mybir.AluOpType
ACT = mybir.ActivationFunctionType
AX = mybir.AxisListType

P = 128
NB = 4
CH = 1024
PX = 1024
G = 2
J = 4
OB = CH // P
PT = 512
NU = NB * PX // PT
EPS = 1e-5
COUNT = NB * PX
FLOPS = 2 * CH * CH * NB * PX

XT_PITCH = 136
N_XT = 4
PIECES = (
    ((0, 0, 1024), (1, 0, 1024), (2, 0, 1024), (3, 0, 1024)),
    ((0, 0, 1024), (1, 0, 1024), (2, 0, 1024), (3, 0, 512), (3, 512, 512)),
)
BN_J = ((0, 1), (0,))
T_BANKS = (5, 6, 7)
WT_BANKS = (5, 6, 7, 0, 1, 5, 6, 7)


def tile_caps_bn_t_kernel(tc, x, weight, bias, out):
    nc = tc.nc
    x_v = x.rearrange("n (g p j) h w -> g n p j (h w)", g=G, p=P, j=J)
    w_v = weight.rearrange("c (p ob) i -> p (c ob) i", ob=OB)
    b_v = bias.rearrange("(p ob) -> p ob", ob=OB)
    out_v = out.rearrange("n (p ob) h w -> n p ob (h w)", ob=OB)

    with ExitStack() as ctx:
        ctx.enter_context(tc.manual_schedule())
        keep = ctx.enter_context(tc.tile_pool(name="keep", bufs=1))
        grp_pool = ctx.enter_context(tc.tile_pool(name="grpp", bufs=4))
        q0_pool = ctx.enter_context(tc.tile_pool(name="q0p", bufs=8))
        q1_pool = ctx.enter_context(tc.tile_pool(name="q1p", bufs=3))
        o_pool = ctx.enter_context(tc.tile_pool(name="op", bufs=6))
        junk_pool = ctx.enter_context(tc.tile_pool(name="junkp", bufs=2))
        psum = ctx.enter_context(tc.psum_pool(name="ps", bufs=1))

        def bank(i, shape, dtype, name):
            return psum.tile(shape, dtype, name=name, tag="b%d" % (i % 8))

        bias_bf = keep.tile([P, OB], BF16, name="bias_bf")
        nc.scalar.dma_start(out=bias_bf[:], in_=b_v)
        xs = [[keep.tile([P, J, PX], BF16, name="x%d%d" % (g, n)) for n in range(NB)] for g in range(G)]
        for g in range(G):
            for k, (n, p0, w) in enumerate(PIECES[g]):
                cuts = ((0, 1), (2, 3), (1, 2), (3, 4)) if (g, k) == (0, 0) else ((0, 2), (2, 4))
                for j0, j1 in cuts:
                    nc.sync.dma_start(
                        out=xs[g][n][:, j0:j1, p0 : p0 + w], in_=x_v[g, n][:, j0:j1, p0 : p0 + w]
                    )
        w_sb = keep.tile([P, OB, CH], BF16, name="w_sb")
        for a in range(OB // 2):
            nc.sync.dma_start(out=w_sb[:, 2 * a : 2 * a + 2, :], in_=w_v[:, 2 * a : 2 * a + 2, :])

        one = keep.tile([P, 1], F32, name="one")
        nc.vector.memset(one[:], 1.0)
        warm = keep.tile([P, 1], F32, name="warm")
        nc.scalar.activation(out=warm[:], in_=one[:], func=ACT.Sqrt)
        ident_f = keep.tile([P, P], F32, name="ident_f")
        make_identity(nc, ident_f[:])
        ident_s = keep.tile([P, P], BF16, name="ident_s")
        nc.vector.tensor_scalar(out=ident_s[:], in0=ident_f[:], scalar1=1.0 / COUNT, scalar2=None, op0=ALU.mult)
        xT = [keep.tile([P, 4, 2 * XT_PITCH], BF16, name="xT%d" % i) for i in range(N_XT)]
        for t in xT:
            nc.vector.memset(t[:, :, 2 * P : 2 * P + 4], 1.0 / COUNT)

        mv = keep.tile([P, G * J, 2], F32, name="mv")
        rstd = keep.tile([P, G * J], F32, name="rstd")
        ex2 = keep.tile([P, G, J], F32, name="ex2")
        m2 = keep.tile([P, G, J], F32, name="m2")
        ve = keep.tile([P, G, J], F32, name="ve")
        sd = [keep.tile([P, J], F32, name="sd%d" % g) for g in range(G)]
        junkf = keep.tile([P, P], F32, name="junkf")
        st = [keep.tile([P, 2, 2 * NB, 6], F32, name="st%d" % g) for g in range(G)]
        acc = keep.tile([P, len(PIECES[1])], F32, name="acc")
        gram = [[bank(2 * g + jj, [P, PT], F32, "gram%d%d" % (g, jj)) for jj in range(2)] for g in range(G)]
        sx_ps = bank(4, [P, PT], F32, "sx_ps")
        counters = {"t": 0, "m": 0}
        moved = {}

        def bn_piece(g, k):
            n, p0, w = PIECES[g][k]
            for j in BN_J[g]:
                for h in range(p0 // PT, (p0 + w) // PT):
                    nc.vector.bn_stats(out=st[g][:, j, 2 * n + h, :], in_=xs[g][n][:, j, PT * h : PT * h + PT])

        def turn_piece(g, k):
            n, p0, w = PIECES[g][k]
            nb = w // (2 * P)
            xw = xs[g][n][:].bitcast(F32)
            for jj in range(2):
                t = counters["t"]
                counters["t"] = t + 1
                tp = bank(T_BANKS[t % len(T_BANKS)], [P, 4, P], F32, "tp")
                for b in range(nb):
                    nc.tensor.transpose(
                        tp[:, b, :], xw[:, 2 + jj, p0 // 2 + P * b : p0 // 2 + P * b + P], ident_f[:]
                    )
                xt = xT[t % N_XT]
                nc.scalar.copy(out=xt[:].bitcast(F32)[:, 0:nb, 0:P], in_=tp[:, 0:nb, :])
                moved[(g, k, jj)] = xt

        def square_piece(g, k):
            n, p0, w = PIECES[g][k]
            junk = junk_pool.tile([P, PX], BF16, name="junk", tag="junk")
            nc.scalar.activation(
                out=junk[:, 0:w],
                in_=xs[g][n][:, 1, p0 : p0 + w],
                func=ACT.Square,
                scale=1.0 / 64.0,
                accum_out=acc[:, k : k + 1],
            )
            for b in range(w // P):
                nc.tensor.matmul(
                    sx_ps[:, 0:P],
                    lhsT=ident_s[:],
                    rhs=xs[g][n][:, 1, p0 + P * b : p0 + P * b + P],
                    start=(k == 0 and b == 0),
                    stop=(k == len(PIECES[g]) - 1 and b == w // P - 1),
                )

        def gram_piece(g, k):
            nb = PIECES[g][k][2] // (2 * P)
            for jj in range(2):
                halves = moved[(g, k, jj)][:].rearrange("p b (c e) -> p b e c", e=2)
                for b in range(nb):
                    for e in range(2):
                        nc.tensor.matmul(
                            gram[g][jj][:, 0 : P + 2],
                            lhsT=halves[:, b, e, 0:P],
                            rhs=halves[:, b, e, 0 : P + 2],
                            start=(k == 0 and b == 0 and e == 0),
                            stop=(k == len(PIECES[g]) - 1 and b == nb - 1 and e == 1),
                        )

        def chain_bn(g):
            lo = len(BN_J[g])
            for j in BN_J[g]:
                nc.vector.bn_aggr(out=mv[:, J * g + j, :], in_=st[g][:, j].rearrange("p a b -> p (a b)"))
            nc.vector.tensor_scalar(
                out=ve[:, g, 0:lo], in0=mv[:, J * g : J * g + lo, 1], scalar1=EPS, scalar2=None, op0=ALU.add
            )

        def chain_a(g):
            lo = len(BN_J[g])
            if g == 1:
                nc.vector.tensor_reduce(out=ex2[:, g, 1:2], in_=acc[:], op=ALU.add, axis=AX.X)
                nc.vector.tensor_reduce(out=mv[:, J * g + 1, 0:1], in_=sx_ps[:, 0:P], op=ALU.add, axis=AX.X)
            for jj in range(2):
                nc.vector.scalar_tensor_tensor(
                    out=junkf[:],
                    in0=gram[g][jj][:, 0:P],
                    scalar=1.0 / COUNT,
                    in1=ident_f[:],
                    op0=ALU.mult,
                    op1=ALU.mult,
                    accum_out=ex2[:, g, 2 + jj : 3 + jj],
                )
                nc.vector.tensor_copy(out=mv[:, J * g + 2 + jj, 0:1], in_=gram[g][jj][:, P : P + 1])
            mean_g = mv[:, J * g + lo : J * g + J, 0]
            nc.vector.tensor_tensor(out=m2[:, g, lo:J], in0=mean_g, in1=mean_g, op=ALU.mult)
            nc.vector.scalar_tensor_tensor(
                out=ve[:, g, lo:J],
                in0=ex2[:, g, lo:J],
                scalar=EPS,
                in1=m2[:, g, lo:J],
                op0=ALU.add,
                op1=ALU.subtract,
            )

        def chain_s(g):
            nc.scalar.activation(out=sd[g][:], in_=ve[:, g, :], func=ACT.Sqrt)

        def chain_b(g):
            nc.vector.reciprocal(out=rstd[:, J * g : J * g + J], in_=sd[g][:])

        wg = keep.tile([P, OB // 2, G, 4 * 2 * P], BF16, name="wg", align_bytes=64)
        wq = keep.tile([P, OB // 2, G, 2 * P], U32, name="wq", align_bytes=64)
        wsc = keep.tile([P, OB // 2, G, 2 * P], U8, name="wsc", align_bytes=64)
        words = w_sb[:].bitcast(F32).rearrange("p ob (g v u) -> p ob g u v", g=G, u=2)

        def w_move(a, gs):
            for g in gs:
                wt = bank(WT_BANKS[2 * a + g], [P, 2, 2, P], F32, "wt")
                for l in range(2):
                    for u in range(2):
                        nc.tensor.transpose(wt[:, l, u, :], words[:, 2 * a + l, g, u, :], ident_f[:])
                nc.scalar.copy(
                    out=wg[:, a, g, :].bitcast(F32).rearrange("p (l o u) -> p l o u", l=2, u=2),
                    in_=wt[:].rearrange("p l u o -> p l o u"),
                )

        def w_quant(a):
            nc.vector.quantize_mx(
                out=wq[:, a].rearrange("p g c -> p (g c)").bitcast(FP8X4),
                scales=wsc[:, a].rearrange("p g c -> p (g c)"),
                in_=wg[:, a].rearrange("p g c -> p (g c)"),
            )

        held = {}

        def norm(g, n, p0, w):
            for j in range(J):
                nc.vector.tensor_scalar(
                    out=xs[g][n][:, j, p0 : p0 + w],
                    in0=xs[g][n][:, j, p0 : p0 + w],
                    scalar1=mv[:, J * g + j, 0:1],
                    scalar2=rstd[:, J * g + j : J * g + j + 1],
                    op0=ALU.subtract,
                    op1=ALU.mult,
                )

        def regroup(g, u):
            n, h = divmod(u, 2)
            grp = grp_pool.tile([P, PT, J], BF16, name="grp", tag="grp", align_bytes=64)
            nc.vector.tensor_copy(
                out=grp[:].rearrange("p (c i) t -> p c t i", i=8),
                in_=xs[g][n][:, :, PT * h : PT * h + PT].rearrange("p t (c i) -> p c t i", i=8),
            )
            held[("grp", g, u)] = grp

        def quant(g, u):
            pool = q0_pool if g == 0 else q1_pool
            q = pool.tile([P, PT], U32, name="xq", tag="xq", align_bytes=64)
            sc = pool.tile([P, PT], U8, name="xsc", tag="xsc", align_bytes=64)
            nc.vector.quantize_mx(
                out=q[:].bitcast(FP8X4), scales=sc[:], in_=held[("grp", g, u)][:].rearrange("p w t -> p (w t)")
            )
            held[("q", g, u)] = (q, sc)

        def multiply(u, a, on_vector=()):
            n, h = divmod(u, 2)
            ot = o_pool.tile([P, 2, PT], F32, name="ot", tag="ot")
            for l in range(2):
                ob = 2 * a + l
                m = counters["m"]
                counters["m"] = m + 1
                acc_ps = bank(m + 2, [P, PT], F32, "mm")
                for g in range(G):
                    q, sc = held[("q", g, u)]
                    nc.tensor.matmul_mx(
                        out=acc_ps[:],
                        lhsT=wq[:, a, g, P * l : P * l + P].bitcast(FP8X4),
                        lhsT_scale=wsc[:, a, g, P * l : P * l + P],
                        rhs=q[:].bitcast(FP8X4),
                        rhs_scale=sc[:],
                        start=(g == 0),
                        stop=(g == G - 1),
                    )
                if l in on_vector:
                    nc.vector.tensor_scalar(
                        out=ot[:, l, :], in0=acc_ps[:], scalar1=bias_bf[:, ob : ob + 1], scalar2=None, op0=ALU.add
                    )
                else:
                    nc.scalar.activation(
                        out=ot[:, l, :], in_=acc_ps[:], func=ACT.Identity, bias=bias_bf[:, ob : ob + 1], scale=1.0
                    )
            nc.sync.dma_start(out=out_v[n][:, 2 * a : 2 * a + 2, PT * h : PT * h + PT], in_=ot[:])

        bn_piece(0, 0)
        turn_piece(0, 0)
        for k in range(1, 4):
            bn_piece(0, k)
            turn_piece(0, k)
            gram_piece(0, k - 1)
        gram_piece(0, 3)
        chain_bn(0)
        bn_piece(1, 0)
        chain_a(0)
        chain_s(0)
        turn_piece(1, 0)
        square_piece(1, 0)
        chain_b(0)
        norm(0, 0, 0, PX)
        bn_piece(1, 1)
        turn_piece(1, 1)
        square_piece(1, 1)
        gram_piece(1, 0)
        regroup(0, 0)
        bn_piece(1, 2)
        turn_piece(1, 2)
        square_piece(1, 2)
        gram_piece(1, 1)
        quant(0, 0)
        regroup(0, 1)
        bn_piece(1, 3)
        turn_piece(1, 3)
        square_piece(1, 3)
        gram_piece(1, 2)
        quant(0, 1)
        bn_piece(1, 4)
        turn_piece(1, 4)
        square_piece(1, 4)
        gram_piece(1, 3)
        gram_piece(1, 4)
        chain_bn(1)
        chain_a(1)
        chain_s(1)
        w_move(0, (0, 1))
        chain_b(1)
        norm(1, 0, 0, PT)
        regroup(1, 0)
        w_quant(0)
        for a in range(1, OB // 2):
            w_move(a, (0, 1))
        quant(1, 0)
        multiply(0, 0)
        w_quant(1)
        multiply(0, 1)
        w_quant(2)
        multiply(0, 2)
        w_quant(3)
        multiply(0, 3)
        norm(1, 0, PT, PT)
        regroup(1, 1)
        quant(1, 1)
        for u in range(1, NU):
            n, h = divmod(u, 2)
            if u + 1 < NU:
                n1, h1 = divmod(u + 1, 2)
                if n1 == NB - 1:
                    norm(0, n1, PT * h1, PT)
                    norm(1, n1, PT * h1, PT)
                elif h1 == 0:
                    norm(0, n1, 0, PX)
                    norm(1, n1, 0, PX)
                regroup(0, u + 1)
                regroup(1, u + 1)
                quant(0, u + 1)
                quant(1, u + 1)
            for a in range(OB // 2):
                multiply(u, a, (1,) if u == NU - 1 else ())
